import numpy as np
import ml_dtypes


def mxq(x, axis, fmt="e4m3"):
    dtype, down = {"e4m3": (ml_dtypes.float8_e4m3fn, 7), "e5m2": (ml_dtypes.float8_e5m2, 14)}[fmt]
    v = np.moveaxis(np.asarray(x, np.float32).astype(ml_dtypes.bfloat16).astype(np.float64), axis, -1)
    blocks = v.reshape(v.shape[:-1] + (-1, 32))
    amax = np.abs(blocks).max(-1, keepdims=True)
    byte = np.maximum(np.where(amax > 0, np.frexp(amax)[1] - 1 + 127, 0) - down, 1)
    scale = np.exp2(byte - 127.0)
    codes = (blocks / scale).astype(np.float32).astype(dtype).astype(np.float64)
    return np.moveaxis((codes * scale).reshape(v.shape), -1, axis)


WIDE = False


def mx_kscale(k):
    if not WIDE:
        return np.ones(k)
    levels = np.array([10, -10, 5, -5, 0])
    a = np.random.permutation(np.resize(levels, k // 512 * 4)).reshape(k // 512, 4)
    idx = np.arange(k)
    return np.exp2(a[idx // 512, idx % 128 // 32])


BF16 = ml_dtypes.bfloat16


def bf(x):
    return np.asarray(x, np.float32).astype(BF16)


def f64(x):
    return np.asarray(x).astype(np.float64)


N, P, D, E, F = 4096, 3, 512, 128, 1024


def setup_inputs():
    s = mx_kscale(D)
    x = np.random.standard_normal((N, P, D)) + 0.5 * np.random.standard_normal((1, P, D))
    return {"x": bf(x * s),
            "w1a": bf(np.random.standard_normal((D, E)) / np.sqrt(D) / s[:, None]),
            "w2a": bf(np.random.standard_normal((D, E)) / np.sqrt(D) / s[:, None])}


def reference(x, w1a, w2a):
    h = f64(x)
    neigh = (h.sum(axis=1, keepdims=True) - h) * 0.5
    return (mxq(h, 2, "e4m3") @ mxq(f64(w2a), 0, "e4m3")) + (mxq(neigh, 2, "e4m3") @ mxq(f64(w1a), 0, "e4m3"))

@@ -1,0 +1,168 @@
+import concourse.mybir as mybir
+from concourse.masks import make_identity
+
+BF16 = mybir.dt.bfloat16
+F32 = mybir.dt.float32
+U32 = mybir.dt.uint32
+U8 = mybir.dt.uint8
+FP8X4 = mybir.dt.float8_e4m3fn_x4
+
+P = 128
+PACK = 4
+ITEMS, HOPS, D, E = 4096, 3, 512, 128
+SLOTS = ITEMS // P
+CHUNK = 2
+CHUNKS = SLOTS // CHUNK
+WORDS = D // 2
+HOP_ROWS = CHUNK * P
+HOP_VALUES = HOP_ROWS * PACK
+AHEAD = 2
+
+FLOPS = 2 * 2 * ITEMS * HOPS * D * E
+
+
+def tile_dogtaitujuanji_pa_t_kernel(tc, x, w1a, w2a, out):
+    nc = tc.nc
+    x_view = x.rearrange("(q s) h d -> q (s h d)", s=SLOTS)
+    out_view = out.rearrange("(q s) h e -> q (s h e)", s=SLOTS)
+
+    with (
+        tc.tile_pool(name="consts", bufs=1) as consts,
+        tc.tile_pool(name="rows", bufs=CHUNKS) as rows_pool,
+        tc.tile_pool(name="grouped", bufs=AHEAD + 1) as grouped_pool,
+        tc.tile_pool(name="work", bufs=2) as work_pool,
+        tc.tile_pool(name="packed", bufs=3) as packed_pool,
+        tc.tile_pool(name="results", bufs=3) as results_pool,
+        tc.psum_pool(name="flipped", bufs=5) as flipped_pool,
+        tc.psum_pool(name="sums", bufs=3) as sums_pool,
+        tc.manual_schedule(),
+    ):
+        x_rows = []
+        for c in range(CHUNKS):
+            rows = rows_pool.tile([P, CHUNK * HOPS * D], BF16)
+            width = CHUNK * HOPS * D
+            nc.sync.dma_start(out=rows[:], in_=x_view[:, c * width : (c + 1) * width])
+            x_rows.append(rows)
+
+        ident = consts.tile([P, P], F32)
+        make_identity(nc, ident[:])
+
+        w_rows = consts.tile([P, 2, PACK, E], BF16)
+        for i, w in enumerate((w2a, w1a)):
+            nc.scalar.dma_start(
+                out=w_rows[:, i, :, :].rearrange("r (u e) c -> r u (e c)", u=2),
+                in_=w.rearrange("(u r e) c -> r u (e c)", u=2, e=2),
+            )
+        w_grouped = consts.tile([P, 2, E, PACK], BF16, align_bytes=64)
+        nc.vector.tensor_copy(out=w_grouped[:], in_=w_rows[:].rearrange("r i t c -> r i c t"))
+        w_codes = consts.tile([P, 2 * E], U32, align_bytes=64)
+        w_scales = consts.tile([P, 2 * E], U8, align_bytes=64)
+        nc.vector.quantize_mx(
+            out=w_codes[:].bitcast(FP8X4),
+            scales=w_scales[:],
+            in_=w_grouped[:].rearrange("r i c t -> r (i c t)"),
+        )
+
+        grouped = {}
+        half_first = {}
+        packed = {}
+
+        def transpose_chunk(c):
+            words = x_rows[c][:].bitcast(F32).rearrange("q (s h w) -> q s h w", s=CHUNK, h=HOPS)
+            x_grouped = grouped_pool.tile([P, HOPS * HOP_VALUES], BF16, align_bytes=64)
+            grouped_words = x_grouped[:].bitcast(F32).rearrange(
+                "r (h s q u) -> r h s q u", h=HOPS, s=CHUNK, q=P
+            )
+            for h in range(HOPS):
+                for s in range(0, CHUNK, 2):
+                    flipped = flipped_pool.tile([P, 2, 2, P], F32)
+                    for j in range(2):
+                        for u in range(2):
+                            nc.tensor.transpose(
+                                out=flipped[:, j, u, :],
+                                in_=words[:, s + j, h, u * P : (u + 1) * P],
+                                identity=ident[:],
+                            )
+                    nc.scalar.copy(
+                        out=grouped_words[:, h, s : s + 2, :, :],
+                        in_=flipped[:].rearrange("r j u q -> r j q u"),
+                    )
+            x_half0 = grouped_pool.tile([P, HOP_VALUES], BF16)
+            nc.scalar.mul(out=x_half0[:], in_=x_grouped[:, 0:HOP_VALUES], mul=0.5)
+            grouped[c] = x_grouped
+            half_first[c] = x_half0
+
+        def quantise_chunk(c):
+            x_grouped = grouped[c]
+            x_half0 = half_first[c]
+            x_codes = packed_pool.tile([P, HOPS * HOP_ROWS], U32, align_bytes=64)
+            x_scales = packed_pool.tile([P, HOPS * HOP_ROWS], U8, align_bytes=64)
+            n_codes = packed_pool.tile([P, HOPS * HOP_ROWS], U32, align_bytes=64)
+            n_scales = packed_pool.tile([P, HOPS * HOP_ROWS], U8, align_bytes=64)
+            x_half12 = work_pool.tile([P, 2 * HOP_VALUES], BF16)
+            neigh = work_pool.tile([P, HOPS * HOP_VALUES], BF16, align_bytes=64)
+            halves = (x_half0[:], x_half12[:, 0:HOP_VALUES], x_half12[:, HOP_VALUES : 2 * HOP_VALUES])
+
+            def quantise_hop(values, codes, scales, h):
+                nc.vector.quantize_mx(
+                    out=codes[:, h * HOP_ROWS : (h + 1) * HOP_ROWS].bitcast(FP8X4),
+                    scales=scales[:, h * HOP_ROWS : (h + 1) * HOP_ROWS],
+                    in_=values[:, h * HOP_VALUES : (h + 1) * HOP_VALUES],
+                )
+
+            quantise_hop(x_grouped, x_codes, x_scales, 0)
+            quantise_hop(x_grouped, x_codes, x_scales, 1)
+            nc.vector.tensor_scalar_mul(
+                out=x_half12[:], in0=x_grouped[:, HOP_VALUES : 3 * HOP_VALUES], scalar1=0.5
+            )
+            quantise_hop(x_grouped, x_codes, x_scales, 2)
+            for h in range(HOPS):
+                nc.vector.tensor_tensor(
+                    out=neigh[:, h * HOP_VALUES : (h + 1) * HOP_VALUES],
+                    in0=halves[(h + 1) % HOPS],
+                    in1=halves[(h + 2) % HOPS],
+                    op=mybir.AluOpType.add,
+                )
+            for h in range(HOPS):
+                quantise_hop(neigh, n_codes, n_scales, h)
+            packed[c] = (x_codes, x_scales, n_codes, n_scales)
+
+        def multiply_chunk(c):
+            x_codes, x_scales, n_codes, n_scales = packed[c]
+            result = results_pool.tile([P, CHUNK, HOPS * E], F32)
+            for s in range(CHUNK):
+                sums = sums_pool.tile([P, HOPS, E], F32)
+                for h in range(HOPS):
+                    cols = slice(h * HOP_ROWS + s * P, h * HOP_ROWS + (s + 1) * P)
+                    nc.tensor.matmul_mx(
+                        out=sums[:, h, :],
+                        lhsT=x_codes[:, cols].bitcast(FP8X4),
+                        lhsT_scale=x_scales[:, cols],
+                        rhs=w_codes[:, 0:E].bitcast(FP8X4),
+                        rhs_scale=w_scales[:, 0:E],
+                        start=True,
+                        stop=False,
+                    )
+                    nc.tensor.matmul_mx(
+                        out=sums[:, h, :],
+                        lhsT=n_codes[:, cols].bitcast(FP8X4),
+                        lhsT_scale=n_scales[:, cols],
+                        rhs=w_codes[:, E : 2 * E].bitcast(FP8X4),
+                        rhs_scale=w_scales[:, E : 2 * E],
+                        start=False,
+                        stop=True,
+                    )
+                nc.scalar.copy(out=result[:, s, :], in_=sums[:].rearrange("q h e -> q (h e)"))
+            width = CHUNK * HOPS * E
+            nc.sync.dma_start(
+                out=out_view[:, c * width : (c + 1) * width],
+                in_=result[:].rearrange("q s v -> q (s v)"),
+            )
+
+        for step in range(CHUNKS + AHEAD):
+            if step < CHUNKS:
+                transpose_chunk(step)
+            if 1 <= step <= CHUNKS:
+                quantise_chunk(step - 1)
+            if step >= AHEAD:
+                multiply_chunk(step - AHEAD)

@@ -23,7 +23,7 @@ FLOPS = 2 * 2 * ITEMS * HOPS * D * E
 
 def tile_dogtaitujuanji_pa_t_kernel(tc, x, w1a, w2a, out):
     nc = tc.nc
-    x_view = x.rearrange("(q s) h d -> q (s h d)", s=SLOTS)
+    x_view = x.rearrange("(q s) h d -> q s h d", s=SLOTS)
     out_view = out.rearrange("(q s) h e -> q (s h e)", s=SLOTS)
 
     with (
@@ -32,27 +32,35 @@ def tile_dogtaitujuanji_pa_t_kernel(tc, x, w1a, w2a, out):
         tc.tile_pool(name="grouped", bufs=AHEAD + 1) as grouped_pool,
         tc.tile_pool(name="work", bufs=2) as work_pool,
         tc.tile_pool(name="packed", bufs=3) as packed_pool,
-        tc.tile_pool(name="results", bufs=3) as results_pool,
+        tc.tile_pool(name="results", bufs=4) as results_pool,
         tc.psum_pool(name="flipped", bufs=5) as flipped_pool,
         tc.psum_pool(name="sums", bufs=3) as sums_pool,
         tc.manual_schedule(),
     ):
-        x_rows = []
-        for c in range(CHUNKS):
-            rows = rows_pool.tile([P, CHUNK * HOPS * D], BF16)
-            width = CHUNK * HOPS * D
-            nc.sync.dma_start(out=rows[:], in_=x_view[:, c * width : (c + 1) * width])
-            x_rows.append(rows)
+        def load_chunk(c, hops_per_load):
+            rows = rows_pool.tile([P, CHUNK, HOPS, D], BF16)
+            for h in range(0, HOPS, hops_per_load):
+                nc.sync.dma_start(
+                    out=rows[:, :, h : h + hops_per_load, :],
+                    in_=x_view[:, c * CHUNK : (c + 1) * CHUNK, h : h + hops_per_load, :],
+                )
+            return rows
+
+        x_rows = [load_chunk(0, 1)]
+
+        w_rows = consts.tile([P, 2, PACK, E], BF16)
+        for i, w in enumerate((w2a, w1a)):
+            nc.sync.dma_start(
+                out=w_rows[:, i, :, :].rearrange("r (u e) c -> r u (e c)", u=2),
+                in_=w.rearrange("(u r e) c -> r u (e c)", u=2, e=2),
+            )
+
+        for c in range(1, CHUNKS):
+            x_rows.append(load_chunk(c, HOPS))
 
         ident = consts.tile([P, P], F32)
         make_identity(nc, ident[:])
 
-        w_rows = consts.tile([P, 2, PACK, E], BF16)
-        for i, w in enumerate((w2a, w1a)):
-            nc.scalar.dma_start(
-                out=w_rows[:, i, :, :].rearrange("r (u e) c -> r u (e c)", u=2),
-                in_=w.rearrange("(u r e) c -> r u (e c)", u=2, e=2),
-            )
         w_grouped = consts.tile([P, 2, E, PACK], BF16, align_bytes=64)
         nc.vector.tensor_copy(out=w_grouped[:], in_=w_rows[:].rearrange("r i t c -> r i c t"))
         w_codes = consts.tile([P, 2 * E], U32, align_bytes=64)
@@ -68,7 +76,12 @@ def tile_dogtaitujuanji_pa_t_kernel(tc, x, w1a, w2a, out):
         packed = {}
 
         def transpose_chunk(c):
-            words = x_rows[c][:].bitcast(F32).rearrange("q (s h w) -> q s h w", s=CHUNK, h=HOPS)
+            words = (
+                x_rows[c][:]
+                .rearrange("q s h d -> q (s h d)")
+                .bitcast(F32)
+                .rearrange("q (s h w) -> q s h w", s=CHUNK, h=HOPS, w=WORDS)
+            )
             x_grouped = grouped_pool.tile([P, HOPS * HOP_VALUES], BF16, align_bytes=64)
             grouped_words = x_grouped[:].bitcast(F32).rearrange(
                 "r (h s q u) -> r h s q u", h=HOPS, s=CHUNK, q=P
@@ -129,13 +142,15 @@ def tile_dogtaitujuanji_pa_t_kernel(tc, x, w1a, w2a, out):
 
         def multiply_chunk(c):
             x_codes, x_scales, n_codes, n_scales = packed[c]
-            result = results_pool.tile([P, CHUNK, HOPS * E], F32)
+            banks = []
             for s in range(CHUNK):
                 sums = sums_pool.tile([P, HOPS, E], F32)
-                for h in range(HOPS):
+                banks.append(sums)
+            for h in range(HOPS):
+                for s in range(CHUNK):
                     cols = slice(h * HOP_ROWS + s * P, h * HOP_ROWS + (s + 1) * P)
                     nc.tensor.matmul_mx(
-                        out=sums[:, h, :],
+                        out=banks[s][:, h, :],
                         lhsT=x_codes[:, cols].bitcast(FP8X4),
                         lhsT_scale=x_scales[:, cols],
                         rhs=w_codes[:, 0:E].bitcast(FP8X4),
@@ -144,7 +159,7 @@ def tile_dogtaitujuanji_pa_t_kernel(tc, x, w1a, w2a, out):
                         stop=False,
                     )
                     nc.tensor.matmul_mx(
-                        out=sums[:, h, :],
+                        out=banks[s][:, h, :],
                         lhsT=n_codes[:, cols].bitcast(FP8X4),
                         lhsT_scale=n_scales[:, cols],
                         rhs=w_codes[:, E : 2 * E].bitcast(FP8X4),
@@ -152,12 +167,13 @@ def tile_dogtaitujuanji_pa_t_kernel(tc, x, w1a, w2a, out):
                         start=False,
                         stop=True,
                     )
-                nc.scalar.copy(out=result[:, s, :], in_=sums[:].rearrange("q h e -> q (h e)"))
-            width = CHUNK * HOPS * E
-            nc.sync.dma_start(
-                out=out_view[:, c * width : (c + 1) * width],
-                in_=result[:].rearrange("q s v -> q (s v)"),
-            )
+            for s in range(CHUNK):
+                result = results_pool.tile([P, HOPS * E], F32)
+                nc.scalar.copy(out=result[:], in_=banks[s][:].rearrange("q h e -> q (h e)"))
+                slot = c * CHUNK + s
+                nc.sync.dma_start(
+                    out=out_view[:, slot * HOPS * E : (slot + 1) * HOPS * E], in_=result[:]
+                )
 
         for step in range(CHUNKS + AHEAD):
             if step < CHUNKS:

@@ -11,83 +11,65 @@ P = 128
 PACK = 4
 ITEMS, HOPS, D, E = 4096, 3, 512, 128
 SLOTS = ITEMS // P
-CHUNK = 2
-CHUNKS = SLOTS // CHUNK
 WORDS = D // 2
-HOP_ROWS = CHUNK * P
-HOP_VALUES = HOP_ROWS * PACK
+
+SHORT, LONG, TAPER = 2, 4, 2
+CHUNK_SLOTS = [SHORT] * TAPER + [LONG] * ((SLOTS - 2 * TAPER * SHORT) // LONG) + [SHORT] * TAPER
+CHUNKS = len(CHUNK_SLOTS)
 AHEAD = 2
+LOAD_AHEAD = 5
 
 FLOPS = 2 * 2 * ITEMS * HOPS * D * E
 
 
 def tile_dogtaitujuanji_pa_t_kernel(tc, x, w1a, w2a, out):
     nc = tc.nc
+    assert sum(CHUNK_SLOTS) == SLOTS
     x_view = x.rearrange("(q s) h d -> q s h d", s=SLOTS)
-    out_view = out.rearrange("(q s) h e -> q (s h e)", s=SLOTS)
+    out_view = out.rearrange("(q s) h e -> q s (h e)", s=SLOTS)
 
     with (
         tc.tile_pool(name="consts", bufs=1) as consts,
-        tc.tile_pool(name="rows", bufs=CHUNKS) as rows_pool,
+        tc.tile_pool(name="rows", bufs=LOAD_AHEAD - AHEAD + 1) as rows_pool,
         tc.tile_pool(name="grouped", bufs=AHEAD + 1) as grouped_pool,
         tc.tile_pool(name="work", bufs=2) as work_pool,
         tc.tile_pool(name="packed", bufs=3) as packed_pool,
         tc.tile_pool(name="results", bufs=4) as results_pool,
-        tc.psum_pool(name="flipped", bufs=5) as flipped_pool,
-        tc.psum_pool(name="sums", bufs=3) as sums_pool,
+        tc.psum_pool(name="flipped", bufs=4) as flipped_pool,
+        tc.psum_pool(name="sums", bufs=LONG) as sums_pool,
         tc.manual_schedule(),
     ):
-        def load_chunk(c, hops_per_load):
-            rows = rows_pool.tile([P, CHUNK, HOPS, D], BF16)
-            for h in range(0, HOPS, hops_per_load):
-                nc.sync.dma_start(
-                    out=rows[:, :, h : h + hops_per_load, :],
-                    in_=x_view[:, c * CHUNK : (c + 1) * CHUNK, h : h + hops_per_load, :],
-                )
-            return rows
-
-        x_rows = [load_chunk(0, 1)]
-
-        w_rows = consts.tile([P, 2, PACK, E], BF16)
-        for i, w in enumerate((w2a, w1a)):
-            nc.sync.dma_start(
-                out=w_rows[:, i, :, :].rearrange("r (u e) c -> r u (e c)", u=2),
-                in_=w.rearrange("(u r e) c -> r u (e c)", u=2, e=2),
-            )
-
-        for c in range(1, CHUNKS):
-            x_rows.append(load_chunk(c, HOPS))
-
-        ident = consts.tile([P, P], F32)
-        make_identity(nc, ident[:])
-
-        w_grouped = consts.tile([P, 2, E, PACK], BF16, align_bytes=64)
-        nc.vector.tensor_copy(out=w_grouped[:], in_=w_rows[:].rearrange("r i t c -> r i c t"))
-        w_codes = consts.tile([P, 2 * E], U32, align_bytes=64)
-        w_scales = consts.tile([P, 2 * E], U8, align_bytes=64)
-        nc.vector.quantize_mx(
-            out=w_codes[:].bitcast(FP8X4),
-            scales=w_scales[:],
-            in_=w_grouped[:].rearrange("r i c t -> r (i c t)"),
-        )
-
+        x_rows = {}
         grouped = {}
         half_first = {}
         packed = {}
 
+        def load_chunk(c, hops_per_load):
+            first = sum(CHUNK_SLOTS[:c])
+            slots = CHUNK_SLOTS[c]
+            rows = rows_pool.tile([P, slots, HOPS, D], BF16)
+            for h in range(0, HOPS, hops_per_load):
+                nc.sync.dma_start(
+                    out=rows[:, :, h : h + hops_per_load, :],
+                    in_=x_view[:, first : first + slots, h : h + hops_per_load, :],
+                )
+            x_rows[c] = rows
+
         def transpose_chunk(c):
+            slots = CHUNK_SLOTS[c]
+            hop_values = slots * P * PACK
             words = (
                 x_rows[c][:]
                 .rearrange("q s h d -> q (s h d)")
                 .bitcast(F32)
-                .rearrange("q (s h w) -> q s h w", s=CHUNK, h=HOPS, w=WORDS)
+                .rearrange("q (s h w) -> q s h w", s=slots, h=HOPS, w=WORDS)
             )
-            x_grouped = grouped_pool.tile([P, HOPS * HOP_VALUES], BF16, align_bytes=64)
+            x_grouped = grouped_pool.tile([P, HOPS * hop_values], BF16, align_bytes=64)
             grouped_words = x_grouped[:].bitcast(F32).rearrange(
-                "r (h s q u) -> r h s q u", h=HOPS, s=CHUNK, q=P
+                "r (h s q u) -> r h s q u", h=HOPS, s=slots, q=P
             )
             for h in range(HOPS):
-                for s in range(0, CHUNK, 2):
+                for s in range(0, slots, 2):
                     flipped = flipped_pool.tile([P, 2, 2, P], F32)
                     for j in range(2):
                         for u in range(2):
@@ -100,38 +82,40 @@ def tile_dogtaitujuanji_pa_t_kernel(tc, x, w1a, w2a, out):
                         out=grouped_words[:, h, s : s + 2, :, :],
                         in_=flipped[:].rearrange("r j u q -> r j q u"),
                     )
-            x_half0 = grouped_pool.tile([P, HOP_VALUES], BF16)
-            nc.scalar.mul(out=x_half0[:], in_=x_grouped[:, 0:HOP_VALUES], mul=0.5)
+            x_half0 = grouped_pool.tile([P, hop_values], BF16)
+            nc.scalar.mul(out=x_half0[:], in_=x_grouped[:, 0:hop_values], mul=0.5)
             grouped[c] = x_grouped
             half_first[c] = x_half0
 
         def quantise_chunk(c):
+            hop_rows = CHUNK_SLOTS[c] * P
+            hop_values = hop_rows * PACK
             x_grouped = grouped[c]
             x_half0 = half_first[c]
-            x_codes = packed_pool.tile([P, HOPS * HOP_ROWS], U32, align_bytes=64)
-            x_scales = packed_pool.tile([P, HOPS * HOP_ROWS], U8, align_bytes=64)
-            n_codes = packed_pool.tile([P, HOPS * HOP_ROWS], U32, align_bytes=64)
-            n_scales = packed_pool.tile([P, HOPS * HOP_ROWS], U8, align_bytes=64)
-            x_half12 = work_pool.tile([P, 2 * HOP_VALUES], BF16)
-            neigh = work_pool.tile([P, HOPS * HOP_VALUES], BF16, align_bytes=64)
-            halves = (x_half0[:], x_half12[:, 0:HOP_VALUES], x_half12[:, HOP_VALUES : 2 * HOP_VALUES])
+            x_codes = packed_pool.tile([P, HOPS * hop_rows], U32, align_bytes=64)
+            x_scales = packed_pool.tile([P, HOPS * hop_rows], U8, align_bytes=64)
+            n_codes = packed_pool.tile([P, HOPS * hop_rows], U32, align_bytes=64)
+            n_scales = packed_pool.tile([P, HOPS * hop_rows], U8, align_bytes=64)
+            x_half12 = work_pool.tile([P, 2 * hop_values], BF16)
+            neigh = work_pool.tile([P, HOPS * hop_values], BF16, align_bytes=64)
+            halves = (x_half0[:], x_half12[:, 0:hop_values], x_half12[:, hop_values : 2 * hop_values])
 
             def quantise_hop(values, codes, scales, h):
                 nc.vector.quantize_mx(
-                    out=codes[:, h * HOP_ROWS : (h + 1) * HOP_ROWS].bitcast(FP8X4),
-                    scales=scales[:, h * HOP_ROWS : (h + 1) * HOP_ROWS],
-                    in_=values[:, h * HOP_VALUES : (h + 1) * HOP_VALUES],
+                    out=codes[:, h * hop_rows : (h + 1) * hop_rows].bitcast(FP8X4),
+                    scales=scales[:, h * hop_rows : (h + 1) * hop_rows],
+                    in_=values[:, h * hop_values : (h + 1) * hop_values],
                 )
 
             quantise_hop(x_grouped, x_codes, x_scales, 0)
             quantise_hop(x_grouped, x_codes, x_scales, 1)
             nc.vector.tensor_scalar_mul(
-                out=x_half12[:], in0=x_grouped[:, HOP_VALUES : 3 * HOP_VALUES], scalar1=0.5
+                out=x_half12[:], in0=x_grouped[:, hop_values : 3 * hop_values], scalar1=0.5
             )
             quantise_hop(x_grouped, x_codes, x_scales, 2)
             for h in range(HOPS):
                 nc.vector.tensor_tensor(
-                    out=neigh[:, h * HOP_VALUES : (h + 1) * HOP_VALUES],
+                    out=neigh[:, h * hop_values : (h + 1) * hop_values],
                     in0=halves[(h + 1) % HOPS],
                     in1=halves[(h + 2) % HOPS],
                     op=mybir.AluOpType.add,
@@ -141,14 +125,16 @@ def tile_dogtaitujuanji_pa_t_kernel(tc, x, w1a, w2a, out):
             packed[c] = (x_codes, x_scales, n_codes, n_scales)
 
         def multiply_chunk(c):
+            first = sum(CHUNK_SLOTS[:c])
+            slots = CHUNK_SLOTS[c]
             x_codes, x_scales, n_codes, n_scales = packed[c]
             banks = []
-            for s in range(CHUNK):
+            for s in range(slots):
                 sums = sums_pool.tile([P, HOPS, E], F32)
                 banks.append(sums)
             for h in range(HOPS):
-                for s in range(CHUNK):
-                    cols = slice(h * HOP_ROWS + s * P, h * HOP_ROWS + (s + 1) * P)
+                for s in range(slots):
+                    cols = slice((h * slots + s) * P, (h * slots + s + 1) * P)
                     nc.tensor.matmul_mx(
                         out=banks[s][:, h, :],
                         lhsT=x_codes[:, cols].bitcast(FP8X4),
@@ -158,6 +144,8 @@ def tile_dogtaitujuanji_pa_t_kernel(tc, x, w1a, w2a, out):
                         start=True,
                         stop=False,
                     )
+                for s in range(slots):
+                    cols = slice((h * slots + s) * P, (h * slots + s + 1) * P)
                     nc.tensor.matmul_mx(
                         out=banks[s][:, h, :],
                         lhsT=n_codes[:, cols].bitcast(FP8X4),
@@ -167,18 +155,38 @@ def tile_dogtaitujuanji_pa_t_kernel(tc, x, w1a, w2a, out):
                         start=False,
                         stop=True,
                     )
-            for s in range(CHUNK):
+            for s in range(slots):
                 result = results_pool.tile([P, HOPS * E], F32)
                 nc.scalar.copy(out=result[:], in_=banks[s][:].rearrange("q h e -> q (h e)"))
-                slot = c * CHUNK + s
-                nc.sync.dma_start(
-                    out=out_view[:, slot * HOPS * E : (slot + 1) * HOPS * E], in_=result[:]
-                )
+                nc.sync.dma_start(out=out_view[:, first + s, :], in_=result[:])
 
-        for step in range(CHUNKS + AHEAD):
-            if step < CHUNKS:
-                transpose_chunk(step)
-            if 1 <= step <= CHUNKS:
-                quantise_chunk(step - 1)
-            if step >= AHEAD:
-                multiply_chunk(step - AHEAD)
+        w_rows = consts.tile([P, 2, PACK, E], BF16)
+        for i, w in enumerate((w2a, w1a)):
+            nc.sync.dma_start(
+                out=w_rows[:, i, :, :].rearrange("r (u e) c -> r u (e c)", u=2),
+                in_=w.rearrange("(u r e) c -> r u (e c)", u=2, e=2),
+            )
+        w_grouped = consts.tile([P, 2, E, PACK], BF16, align_bytes=64)
+        nc.vector.tensor_copy(out=w_grouped[:], in_=w_rows[:].rearrange("r i t c -> r i c t"))
+        w_codes = consts.tile([P, 2 * E], U32, align_bytes=64)
+        w_scales = consts.tile([P, 2 * E], U8, align_bytes=64)
+        nc.vector.quantize_mx(
+            out=w_codes[:].bitcast(FP8X4),
+            scales=w_scales[:],
+            in_=w_grouped[:].rearrange("r i c t -> r (i c t)"),
+        )
+        ident = consts.tile([P, P], F32)
+        make_identity(nc, ident[:])
+
+        load_chunk(0, 1)
+        for c in range(1, LOAD_AHEAD):
+            load_chunk(c, HOPS)
+        for c in range(AHEAD):
+            transpose_chunk(c)
+        for c in range(CHUNKS):
+            if c + LOAD_AHEAD < CHUNKS:
+                load_chunk(c + LOAD_AHEAD, HOPS)
+            if c + AHEAD < CHUNKS:
+                transpose_chunk(c + AHEAD)
+            quantise_chunk(c)
+            multiply_chunk(c)

@@ -18,6 +18,7 @@ CHUNK_SLOTS = [SHORT] * TAPER + [LONG] * ((SLOTS - 2 * TAPER * SHORT) // LONG) +
 CHUNKS = len(CHUNK_SLOTS)
 AHEAD = 2
 LOAD_AHEAD = 5
+SCALAR_TWELFTHS = 5
 
 FLOPS = 2 * 2 * ITEMS * HOPS * D * E
 
@@ -41,7 +42,7 @@ def tile_dogtaitujuanji_pa_t_kernel(tc, x, w1a, w2a, out):
     ):
         x_rows = {}
         grouped = {}
-        half_first = {}
+        halved = {}
         packed = {}
 
         def load_chunk(c, hops_per_load):
@@ -82,23 +83,22 @@ def tile_dogtaitujuanji_pa_t_kernel(tc, x, w1a, w2a, out):
                         out=grouped_words[:, h, s : s + 2, :, :],
                         in_=flipped[:].rearrange("r j u q -> r j q u"),
                     )
-            x_half0 = grouped_pool.tile([P, hop_values], BF16)
-            nc.scalar.mul(out=x_half0[:], in_=x_grouped[:, 0:hop_values], mul=0.5)
+            x_half = grouped_pool.tile([P, HOPS * hop_values], BF16)
+            split = HOPS * hop_values * SCALAR_TWELFTHS // 12
+            nc.scalar.mul(out=x_half[:, 0:split], in_=x_grouped[:, 0:split], mul=0.5)
             grouped[c] = x_grouped
-            half_first[c] = x_half0
+            halved[c] = x_half
 
         def quantise_chunk(c):
             hop_rows = CHUNK_SLOTS[c] * P
             hop_values = hop_rows * PACK
             x_grouped = grouped[c]
-            x_half0 = half_first[c]
+            x_half = halved[c]
             x_codes = packed_pool.tile([P, HOPS * hop_rows], U32, align_bytes=64)
             x_scales = packed_pool.tile([P, HOPS * hop_rows], U8, align_bytes=64)
             n_codes = packed_pool.tile([P, HOPS * hop_rows], U32, align_bytes=64)
             n_scales = packed_pool.tile([P, HOPS * hop_rows], U8, align_bytes=64)
-            x_half12 = work_pool.tile([P, 2 * hop_values], BF16)
             neigh = work_pool.tile([P, HOPS * hop_values], BF16, align_bytes=64)
-            halves = (x_half0[:], x_half12[:, 0:hop_values], x_half12[:, hop_values : 2 * hop_values])
 
             def quantise_hop(values, codes, scales, h):
                 nc.vector.quantize_mx(
@@ -109,15 +109,19 @@ def tile_dogtaitujuanji_pa_t_kernel(tc, x, w1a, w2a, out):
 
             quantise_hop(x_grouped, x_codes, x_scales, 0)
             quantise_hop(x_grouped, x_codes, x_scales, 1)
+            split = HOPS * hop_values * SCALAR_TWELFTHS // 12
             nc.vector.tensor_scalar_mul(
-                out=x_half12[:], in0=x_grouped[:, hop_values : 3 * hop_values], scalar1=0.5
+                out=x_half[:, split : HOPS * hop_values],
+                in0=x_grouped[:, split : HOPS * hop_values],
+                scalar1=0.5,
             )
             quantise_hop(x_grouped, x_codes, x_scales, 2)
             for h in range(HOPS):
+                a, b = (h + 1) % HOPS, (h + 2) % HOPS
                 nc.vector.tensor_tensor(
                     out=neigh[:, h * hop_values : (h + 1) * hop_values],
-                    in0=halves[(h + 1) % HOPS],
-                    in1=halves[(h + 2) % HOPS],
+                    in0=x_half[:, a * hop_values : (a + 1) * hop_values],
+                    in1=x_half[:, b * hop_values : (b + 1) * hop_values],
                     op=mybir.AluOpType.add,
                 )
             for h in range(HOPS):

@@ -20,6 +20,14 @@ AHEAD = 2
 LOAD_AHEAD = 5
 SCALAR_TWELFTHS = 5
 
+
+def scalar_share(c, values):
+    if c < TAPER:
+        return 0
+    if c >= CHUNKS - TAPER:
+        return values
+    return values * SCALAR_TWELFTHS // 12
+
 FLOPS = 2 * 2 * ITEMS * HOPS * D * E
 
 
@@ -84,8 +92,9 @@ def tile_dogtaitujuanji_pa_t_kernel(tc, x, w1a, w2a, out):
                         in_=flipped[:].rearrange("r j u q -> r j q u"),
                     )
             x_half = grouped_pool.tile([P, HOPS * hop_values], BF16)
-            split = HOPS * hop_values * SCALAR_TWELFTHS // 12
-            nc.scalar.mul(out=x_half[:, 0:split], in_=x_grouped[:, 0:split], mul=0.5)
+            split = scalar_share(c, HOPS * hop_values)
+            if split > 0:
+                nc.scalar.mul(out=x_half[:, 0:split], in_=x_grouped[:, 0:split], mul=0.5)
             grouped[c] = x_grouped
             halved[c] = x_half
 
@@ -109,12 +118,13 @@ def tile_dogtaitujuanji_pa_t_kernel(tc, x, w1a, w2a, out):
 
             quantise_hop(x_grouped, x_codes, x_scales, 0)
             quantise_hop(x_grouped, x_codes, x_scales, 1)
-            split = HOPS * hop_values * SCALAR_TWELFTHS // 12
-            nc.vector.tensor_scalar_mul(
-                out=x_half[:, split : HOPS * hop_values],
-                in0=x_grouped[:, split : HOPS * hop_values],
-                scalar1=0.5,
-            )
+            split = scalar_share(c, HOPS * hop_values)
+            if split < HOPS * hop_values:
+                nc.vector.tensor_scalar_mul(
+                    out=x_half[:, split : HOPS * hop_values],
+                    in0=x_grouped[:, split : HOPS * hop_values],
+                    scalar1=0.5,
+                )
             quantise_hop(x_grouped, x_codes, x_scales, 2)
             for h in range(HOPS):
                 a, b = (h + 1) % HOPS, (h + 2) % HOPS

@@ -43,7 +43,7 @@ def tile_dogtaitujuanji_pa_t_kernel(tc, x, w1a, w2a, out):
         tc.tile_pool(name="grouped", bufs=AHEAD + 1) as grouped_pool,
         tc.tile_pool(name="work", bufs=2) as work_pool,
         tc.tile_pool(name="packed", bufs=3) as packed_pool,
-        tc.tile_pool(name="results", bufs=4) as results_pool,
+        tc.tile_pool(name="results", bufs=3) as results_pool,
         tc.psum_pool(name="flipped", bufs=4) as flipped_pool,
         tc.psum_pool(name="sums", bufs=LONG) as sums_pool,
         tc.manual_schedule(),
@@ -109,15 +109,16 @@ def tile_dogtaitujuanji_pa_t_kernel(tc, x, w1a, w2a, out):
             n_scales = packed_pool.tile([P, HOPS * hop_rows], U8, align_bytes=64)
             neigh = work_pool.tile([P, HOPS * hop_values], BF16, align_bytes=64)
 
-            def quantise_hop(values, codes, scales, h):
+            def quantise_hops(values, codes, scales, first_hop, hops):
                 nc.vector.quantize_mx(
-                    out=codes[:, h * hop_rows : (h + 1) * hop_rows].bitcast(FP8X4),
-                    scales=scales[:, h * hop_rows : (h + 1) * hop_rows],
-                    in_=values[:, h * hop_values : (h + 1) * hop_values],
+                    out=codes[:, first_hop * hop_rows : (first_hop + hops) * hop_rows].bitcast(FP8X4),
+                    scales=scales[:, first_hop * hop_rows : (first_hop + hops) * hop_rows],
+                    in_=values[:, first_hop * hop_values : (first_hop + hops) * hop_values],
                 )
 
-            quantise_hop(x_grouped, x_codes, x_scales, 0)
-            quantise_hop(x_grouped, x_codes, x_scales, 1)
+            runs = [(0, 1), (1, 1), (2, 1)] if c == 0 else [(0, 2), (2, 1)]
+            for first_hop, hops in runs[:-1]:
+                quantise_hops(x_grouped, x_codes, x_scales, first_hop, hops)
             split = scalar_share(c, HOPS * hop_values)
             if split < HOPS * hop_values:
                 nc.vector.tensor_scalar_mul(
@@ -125,54 +126,53 @@ def tile_dogtaitujuanji_pa_t_kernel(tc, x, w1a, w2a, out):
                     in0=x_grouped[:, split : HOPS * hop_values],
                     scalar1=0.5,
                 )
-            quantise_hop(x_grouped, x_codes, x_scales, 2)
-            for h in range(HOPS):
-                a, b = (h + 1) % HOPS, (h + 2) % HOPS
+            quantise_hops(x_grouped, x_codes, x_scales, runs[-1][0], runs[-1][1])
+            for first_hop, hops in runs:
+                other = (first_hop + 1) % HOPS
                 nc.vector.tensor_tensor(
-                    out=neigh[:, h * hop_values : (h + 1) * hop_values],
-                    in0=x_half[:, a * hop_values : (a + 1) * hop_values],
-                    in1=x_half[:, b * hop_values : (b + 1) * hop_values],
+                    out=neigh[:, first_hop * hop_values : (first_hop + hops) * hop_values],
+                    in0=x_half[:, first_hop * hop_values : (first_hop + hops) * hop_values],
+                    in1=x_half[:, other * hop_values : (other + hops) * hop_values],
                     op=mybir.AluOpType.add,
                 )
-            for h in range(HOPS):
-                quantise_hop(neigh, n_codes, n_scales, h)
+            for first_hop, hops in runs:
+                quantise_hops(neigh, n_codes, n_scales, first_hop, hops)
             packed[c] = (x_codes, x_scales, n_codes, n_scales)
 
         def multiply_chunk(c):
             first = sum(CHUNK_SLOTS[:c])
             slots = CHUNK_SLOTS[c]
             x_codes, x_scales, n_codes, n_scales = packed[c]
-            banks = []
-            for s in range(slots):
-                sums = sums_pool.tile([P, HOPS, E], F32)
-                banks.append(sums)
-            for h in range(HOPS):
+            result = results_pool.tile([P, slots, HOPS, E], F32)
+            for h in (2, 0, 1):
+                place = (h + 1) % HOPS
+                sums = sums_pool.tile([P, LONG, E], F32)
                 for s in range(slots):
-                    cols = slice((h * slots + s) * P, (h * slots + s + 1) * P)
+                    x_cols = slice((h * slots + s) * P, (h * slots + s + 1) * P)
+                    n_cols = slice((place * slots + s) * P, (place * slots + s + 1) * P)
                     nc.tensor.matmul_mx(
-                        out=banks[s][:, h, :],
-                        lhsT=x_codes[:, cols].bitcast(FP8X4),
-                        lhsT_scale=x_scales[:, cols],
+                        out=sums[:, s, :],
+                        lhsT=x_codes[:, x_cols].bitcast(FP8X4),
+                        lhsT_scale=x_scales[:, x_cols],
                         rhs=w_codes[:, 0:E].bitcast(FP8X4),
                         rhs_scale=w_scales[:, 0:E],
                         start=True,
                         stop=False,
                     )
-                for s in range(slots):
-                    cols = slice((h * slots + s) * P, (h * slots + s + 1) * P)
                     nc.tensor.matmul_mx(
-                        out=banks[s][:, h, :],
-                        lhsT=n_codes[:, cols].bitcast(FP8X4),
-                        lhsT_scale=n_scales[:, cols],
+                        out=sums[:, s, :],
+                        lhsT=n_codes[:, n_cols].bitcast(FP8X4),
+                        lhsT_scale=n_scales[:, n_cols],
                         rhs=w_codes[:, E : 2 * E].bitcast(FP8X4),
                         rhs_scale=w_scales[:, E : 2 * E],
                         start=False,
                         stop=True,
                     )
-            for s in range(slots):
-                result = results_pool.tile([P, HOPS * E], F32)
-                nc.scalar.copy(out=result[:], in_=banks[s][:].rearrange("q h e -> q (h e)"))
-                nc.sync.dma_start(out=out_view[:, first + s, :], in_=result[:])
+                nc.scalar.copy(out=result[:, :, h, :], in_=sums[:, 0:slots, :])
+            nc.sync.dma_start(
+                out=out_view[:, first : first + slots, :],
+                in_=result[:].rearrange("q s h e -> q s (h e)"),
+            )
 
         w_rows = consts.tile([P, 2, PACK, E], BF16)
         for i, w in enumerate((w2a, w1a)):

@@ -13,18 +13,21 @@ ITEMS, HOPS, D, E = 4096, 3, 512, 128
 SLOTS = ITEMS // P
 WORDS = D // 2
 
-SHORT, LONG, TAPER = 2, 4, 2
-CHUNK_SLOTS = [SHORT] * TAPER + [LONG] * ((SLOTS - 2 * TAPER * SHORT) // LONG) + [SHORT] * TAPER
+LONG = 4
+HEAD_SLOTS = [1, 1, 2]
+TAIL_SLOTS = [2, 1, 1]
+CHUNK_SLOTS = HEAD_SLOTS + [LONG] * ((SLOTS - sum(HEAD_SLOTS) - sum(TAIL_SLOTS)) // LONG) + TAIL_SLOTS
 CHUNKS = len(CHUNK_SLOTS)
+BANK_SLOTS = 2
 AHEAD = 2
 LOAD_AHEAD = 5
 SCALAR_TWELFTHS = 5
 
 
 def scalar_share(c, values):
-    if c < TAPER:
+    if c < len(HEAD_SLOTS):
         return 0
-    if c >= CHUNKS - TAPER:
+    if c >= CHUNKS - len(TAIL_SLOTS):
         return values
     return values * SCALAR_TWELFTHS // 12
 
@@ -78,9 +81,10 @@ def tile_dogtaitujuanji_pa_t_kernel(tc, x, w1a, w2a, out):
                 "r (h s q u) -> r h s q u", h=HOPS, s=slots, q=P
             )
             for h in range(HOPS):
-                for s in range(0, slots, 2):
-                    flipped = flipped_pool.tile([P, 2, 2, P], F32)
-                    for j in range(2):
+                for s in range(0, slots, BANK_SLOTS):
+                    together = min(BANK_SLOTS, slots - s)
+                    flipped = flipped_pool.tile([P, BANK_SLOTS, 2, P], F32)
+                    for j in range(together):
                         for u in range(2):
                             nc.tensor.transpose(
                                 out=flipped[:, j, u, :],
@@ -88,8 +92,8 @@ def tile_dogtaitujuanji_pa_t_kernel(tc, x, w1a, w2a, out):
                                 identity=ident[:],
                             )
                     nc.scalar.copy(
-                        out=grouped_words[:, h, s : s + 2, :, :],
-                        in_=flipped[:].rearrange("r j u q -> r j q u"),
+                        out=grouped_words[:, h, s : s + together, :, :],
+                        in_=flipped[:, 0:together, :, :].rearrange("r j u q -> r j q u"),
                     )
             x_half = grouped_pool.tile([P, HOPS * hop_values], BF16)
             split = scalar_share(c, HOPS * hop_values)

@@ -15,13 +15,14 @@ WORDS = D // 2
 
 LONG = 4
 HEAD_SLOTS = [1, 1, 2]
-TAIL_SLOTS = [2, 1, 1]
+TAIL_SLOTS = [3, 1]
 CHUNK_SLOTS = HEAD_SLOTS + [LONG] * ((SLOTS - sum(HEAD_SLOTS) - sum(TAIL_SLOTS)) // LONG) + TAIL_SLOTS
 CHUNKS = len(CHUNK_SLOTS)
 BANK_SLOTS = 2
+MEANS_CHUNK = CHUNKS - 2
 AHEAD = 2
 LOAD_AHEAD = 5
-SCALAR_TWELFTHS = 5
+SCALAR_TWELFTHS = 4
 
 
 def scalar_share(c, values):
@@ -95,12 +96,29 @@ def tile_dogtaitujuanji_pa_t_kernel(tc, x, w1a, w2a, out):
                         out=grouped_words[:, h, s : s + together, :, :],
                         in_=flipped[:, 0:together, :, :].rearrange("r j u q -> r j q u"),
                     )
-            x_half = grouped_pool.tile([P, HOPS * hop_values], BF16)
+            grouped[c] = x_grouped
+            x_half = grouped_pool.tile([P, HOPS * hop_values], BF16, align_bytes=64)
+            halved[c] = x_half
+            if c == MEANS_CHUNK:
+                means = x_half[:].rearrange("r (i s q t) -> r i s q t", i=HOPS, s=slots, q=P)
+                for i in range(HOPS):
+                    for s in range(slots):
+                        summed = flipped_pool.tile([P, PACK, P], F32, tag="flipped")
+                        for t in range(PACK):
+                            first_k = (t // 2) * (D // 2) + t % 2
+                            for j, h in enumerate((i, (i + 1) % HOPS)):
+                                nc.tensor.matmul(
+                                    out=summed[:, t, :],
+                                    lhsT=x_rows[c][:, s, h, first_k : (t // 2 + 1) * (D // 2) : 2],
+                                    rhs=half_ident[:],
+                                    start=(j == 0),
+                                    stop=(j == 1),
+                                )
+                        nc.scalar.copy(out=means[:, i, s, :, :], in_=summed[:].rearrange("r t q -> r q t"))
+                return
             split = scalar_share(c, HOPS * hop_values)
             if split > 0:
                 nc.scalar.mul(out=x_half[:, 0:split], in_=x_grouped[:, 0:split], mul=0.5)
-            grouped[c] = x_grouped
-            halved[c] = x_half
 
         def quantise_chunk(c):
             hop_rows = CHUNK_SLOTS[c] * P
@@ -111,6 +129,21 @@ def tile_dogtaitujuanji_pa_t_kernel(tc, x, w1a, w2a, out):
             x_scales = packed_pool.tile([P, HOPS * hop_rows], U8, align_bytes=64)
             n_codes = packed_pool.tile([P, HOPS * hop_rows], U32, align_bytes=64)
             n_scales = packed_pool.tile([P, HOPS * hop_rows], U8, align_bytes=64)
+            packed[c] = (x_codes, x_scales, n_codes, n_scales)
+
+            def quantise_run(values, codes, scales, start, count):
+                nc.vector.quantize_mx(
+                    out=codes[:, start // PACK : (start + count) // PACK].bitcast(FP8X4),
+                    scales=scales[:, start // PACK : (start + count) // PACK],
+                    in_=values[:, start : start + count],
+                )
+
+            if c == MEANS_CHUNK:
+                widest = 4096
+                for values, codes, scales in ((x_grouped, x_codes, x_scales), (x_half, n_codes, n_scales)):
+                    quantise_run(values, codes, scales, 0, widest)
+                    quantise_run(values, codes, scales, widest, HOPS * hop_values - widest)
+                return
             neigh = work_pool.tile([P, HOPS * hop_values], BF16, align_bytes=64)
 
             def quantise_hops(values, codes, scales, first_hop, hops):
@@ -141,7 +174,6 @@ def tile_dogtaitujuanji_pa_t_kernel(tc, x, w1a, w2a, out):
                 )
             for first_hop, hops in runs:
                 quantise_hops(neigh, n_codes, n_scales, first_hop, hops)
-            packed[c] = (x_codes, x_scales, n_codes, n_scales)
 
         def multiply_chunk(c):
             first = sum(CHUNK_SLOTS[:c])
@@ -195,6 +227,8 @@ def tile_dogtaitujuanji_pa_t_kernel(tc, x, w1a, w2a, out):
         )
         ident = consts.tile([P, P], F32)
         make_identity(nc, ident[:])
+        half_ident = consts.tile([P, P], BF16)
+        nc.scalar.mul(out=half_ident[:], in_=ident[:], mul=0.5)
 
         load_chunk(0, 1)
         for c in range(1, LOAD_AHEAD):

@@ -180,30 +180,44 @@ def tile_dogtaitujuanji_pa_t_kernel(tc, x, w1a, w2a, out):
             slots = CHUNK_SLOTS[c]
             x_codes, x_scales, n_codes, n_scales = packed[c]
             result = results_pool.tile([P, slots, HOPS, E], F32)
-            for h in (2, 0, 1):
+
+            def multiply(sums, h, s):
                 place = (h + 1) % HOPS
+                x_cols = slice((h * slots + s) * P, (h * slots + s + 1) * P)
+                n_cols = slice((place * slots + s) * P, (place * slots + s + 1) * P)
+                nc.tensor.matmul_mx(
+                    out=sums,
+                    lhsT=x_codes[:, x_cols].bitcast(FP8X4),
+                    lhsT_scale=x_scales[:, x_cols],
+                    rhs=w_codes[:, 0:E].bitcast(FP8X4),
+                    rhs_scale=w_scales[:, 0:E],
+                    start=True,
+                    stop=False,
+                )
+                nc.tensor.matmul_mx(
+                    out=sums,
+                    lhsT=n_codes[:, n_cols].bitcast(FP8X4),
+                    lhsT_scale=n_scales[:, n_cols],
+                    rhs=w_codes[:, E : 2 * E].bitcast(FP8X4),
+                    rhs_scale=w_scales[:, E : 2 * E],
+                    start=False,
+                    stop=True,
+                )
+
+            if c == MEANS_CHUNK:
+                for s in range(slots):
+                    sums = sums_pool.tile([P, LONG, E], F32)
+                    for h in range(HOPS):
+                        multiply(sums[:, h, :], h, s)
+                    nc.scalar.copy(out=result[:, s, :, :], in_=sums[:, 0:HOPS, :])
+                    nc.sync.dma_start(
+                        out=out_view[:, first + s, :], in_=result[:, s, :, :].rearrange("q h e -> q (h e)")
+                    )
+                return
+            for h in (2, 0, 1):
                 sums = sums_pool.tile([P, LONG, E], F32)
                 for s in range(slots):
-                    x_cols = slice((h * slots + s) * P, (h * slots + s + 1) * P)
-                    n_cols = slice((place * slots + s) * P, (place * slots + s + 1) * P)
-                    nc.tensor.matmul_mx(
-                        out=sums[:, s, :],
-                        lhsT=x_codes[:, x_cols].bitcast(FP8X4),
-                        lhsT_scale=x_scales[:, x_cols],
-                        rhs=w_codes[:, 0:E].bitcast(FP8X4),
-                        rhs_scale=w_scales[:, 0:E],
-                        start=True,
-                        stop=False,
-                    )
-                    nc.tensor.matmul_mx(
-                        out=sums[:, s, :],
-                        lhsT=n_codes[:, n_cols].bitcast(FP8X4),
-                        lhsT_scale=n_scales[:, n_cols],
-                        rhs=w_codes[:, E : 2 * E].bitcast(FP8X4),
-                        rhs_scale=w_scales[:, E : 2 * E],
-                        start=False,
-                        stop=True,
-                    )
+                    multiply(sums[:, s, :], h, s)
                 nc.scalar.copy(out=result[:, :, h, :], in_=sums[:, 0:slots, :])
             nc.sync.dma_start(
                 out=out_view[:, first : first + slots, :],

import concourse.mybir as mybir
from concourse.masks import make_identity

BF16 = mybir.dt.bfloat16
F32 = mybir.dt.float32
U32 = mybir.dt.uint32
U8 = mybir.dt.uint8
FP8X4 = mybir.dt.float8_e4m3fn_x4

P = 128
PACK = 4
ITEMS, HOPS, D, E = 4096, 3, 512, 128
SLOTS = ITEMS // P
WORDS = D // 2

LONG = 4
HEAD_SLOTS = [1, 1, 2]
TAIL_SLOTS = [3, 1]
CHUNK_SLOTS = HEAD_SLOTS + [LONG] * ((SLOTS - sum(HEAD_SLOTS) - sum(TAIL_SLOTS)) // LONG) + TAIL_SLOTS
CHUNKS = len(CHUNK_SLOTS)
BANK_SLOTS = 2
MEANS_CHUNK = CHUNKS - 2
AHEAD = 2
LOAD_AHEAD = 5
SCALAR_TWELFTHS = 4


def scalar_share(c, values):
    if c < len(HEAD_SLOTS):
        return 0
    if c >= CHUNKS - len(TAIL_SLOTS):
        return values
    return values * SCALAR_TWELFTHS // 12

FLOPS = 2 * 2 * ITEMS * HOPS * D * E


def tile_dogtaitujuanji_pa_t_kernel(tc, x, w1a, w2a, out):
    nc = tc.nc
    assert sum(CHUNK_SLOTS) == SLOTS
    x_view = x.rearrange("(q s) h d -> q s h d", s=SLOTS)
    out_view = out.rearrange("(q s) h e -> q s (h e)", s=SLOTS)

    with (
        tc.tile_pool(name="consts", bufs=1) as consts,
        tc.tile_pool(name="rows", bufs=LOAD_AHEAD - AHEAD + 1) as rows_pool,
        tc.tile_pool(name="grouped", bufs=AHEAD + 1) as grouped_pool,
        tc.tile_pool(name="work", bufs=2) as work_pool,
        tc.tile_pool(name="packed", bufs=3) as packed_pool,
        tc.tile_pool(name="results", bufs=3) as results_pool,
        tc.psum_pool(name="flipped", bufs=4) as flipped_pool,
        tc.psum_pool(name="sums", bufs=LONG) as sums_pool,
        tc.manual_schedule(),
    ):
        x_rows = {}
        grouped = {}
        halved = {}
        packed = {}

        def load_chunk(c, hops_per_load):
            first = sum(CHUNK_SLOTS[:c])
            slots = CHUNK_SLOTS[c]
            rows = rows_pool.tile([P, slots, HOPS, D], BF16)
            for h in range(0, HOPS, hops_per_load):
                nc.sync.dma_start(
                    out=rows[:, :, h : h + hops_per_load, :],
                    in_=x_view[:, first : first + slots, h : h + hops_per_load, :],
                )
            x_rows[c] = rows

        def transpose_chunk(c):
            slots = CHUNK_SLOTS[c]
            hop_values = slots * P * PACK
            words = (
                x_rows[c][:]
                .rearrange("q s h d -> q (s h d)")
                .bitcast(F32)
                .rearrange("q (s h w) -> q s h w", s=slots, h=HOPS, w=WORDS)
            )
            x_grouped = grouped_pool.tile([P, HOPS * hop_values], BF16, align_bytes=64)
            grouped_words = x_grouped[:].bitcast(F32).rearrange(
                "r (h s q u) -> r h s q u", h=HOPS, s=slots, q=P
            )
            for h in range(HOPS):
                for s in range(0, slots, BANK_SLOTS):
                    together = min(BANK_SLOTS, slots - s)
                    flipped = flipped_pool.tile([P, BANK_SLOTS, 2, P], F32)
                    for j in range(together):
                        for u in range(2):
                            nc.tensor.transpose(
                                out=flipped[:, j, u, :],
                                in_=words[:, s + j, h, u * P : (u + 1) * P],
                                identity=ident[:],
                            )
                    nc.scalar.copy(
                        out=grouped_words[:, h, s : s + together, :, :],
                        in_=flipped[:, 0:together, :, :].rearrange("r j u q -> r j q u"),
                    )
            grouped[c] = x_grouped
            x_half = grouped_pool.tile([P, HOPS * hop_values], BF16, align_bytes=64)
            halved[c] = x_half
            if c == MEANS_CHUNK:
                means = x_half[:].rearrange("r (i s q t) -> r i s q t", i=HOPS, s=slots, q=P)
                for i in range(HOPS):
                    for s in range(slots):
                        summed = flipped_pool.tile([P, PACK, P], F32, tag="flipped")
                        for t in range(PACK):
                            first_k = (t // 2) * (D // 2) + t % 2
                            for j, h in enumerate((i, (i + 1) % HOPS)):
                                nc.tensor.matmul(
                                    out=summed[:, t, :],
                                    lhsT=x_rows[c][:, s, h, first_k : (t // 2 + 1) * (D // 2) : 2],
                                    rhs=half_ident[:],
                                    start=(j == 0),
                                    stop=(j == 1),
                                )
                        nc.scalar.copy(out=means[:, i, s, :, :], in_=summed[:].rearrange("r t q -> r q t"))
                return
            split = scalar_share(c, HOPS * hop_values)
            if split > 0:
                nc.scalar.mul(out=x_half[:, 0:split], in_=x_grouped[:, 0:split], mul=0.5)

        def quantise_chunk(c):
            hop_rows = CHUNK_SLOTS[c] * P
            hop_values = hop_rows * PACK
            x_grouped = grouped[c]
            x_half = halved[c]
            x_codes = packed_pool.tile([P, HOPS * hop_rows], U32, align_bytes=64)
            x_scales = packed_pool.tile([P, HOPS * hop_rows], U8, align_bytes=64)
            n_codes = packed_pool.tile([P, HOPS * hop_rows], U32, align_bytes=64)
            n_scales = packed_pool.tile([P, HOPS * hop_rows], U8, align_bytes=64)
            packed[c] = (x_codes, x_scales, n_codes, n_scales)

            def quantise_run(values, codes, scales, start, count):
                nc.vector.quantize_mx(
                    out=codes[:, start // PACK : (start + count) // PACK].bitcast(FP8X4),
                    scales=scales[:, start // PACK : (start + count) // PACK],
                    in_=values[:, start : start + count],
                )

            if c == MEANS_CHUNK:
                widest = 4096
                for values, codes, scales in ((x_grouped, x_codes, x_scales), (x_half, n_codes, n_scales)):
                    quantise_run(values, codes, scales, 0, widest)
                    quantise_run(values, codes, scales, widest, HOPS * hop_values - widest)
                return
            neigh = work_pool.tile([P, HOPS * hop_values], BF16, align_bytes=64)

            def quantise_hops(values, codes, scales, first_hop, hops):
                nc.vector.quantize_mx(
                    out=codes[:, first_hop * hop_rows : (first_hop + hops) * hop_rows].bitcast(FP8X4),
                    scales=scales[:, first_hop * hop_rows : (first_hop + hops) * hop_rows],
                    in_=values[:, first_hop * hop_values : (first_hop + hops) * hop_values],
                )

            runs = [(0, 1), (1, 1), (2, 1)] if c == 0 else [(0, 2), (2, 1)]
            for first_hop, hops in runs[:-1]:
                quantise_hops(x_grouped, x_codes, x_scales, first_hop, hops)
            split = scalar_share(c, HOPS * hop_values)
            if split < HOPS * hop_values:
                nc.vector.tensor_scalar_mul(
                    out=x_half[:, split : HOPS * hop_values],
                    in0=x_grouped[:, split : HOPS * hop_values],
                    scalar1=0.5,
                )
            quantise_hops(x_grouped, x_codes, x_scales, runs[-1][0], runs[-1][1])
            for first_hop, hops in runs:
                other = (first_hop + 1) % HOPS
                nc.vector.tensor_tensor(
                    out=neigh[:, first_hop * hop_values : (first_hop + hops) * hop_values],
                    in0=x_half[:, first_hop * hop_values : (first_hop + hops) * hop_values],
                    in1=x_half[:, other * hop_values : (other + hops) * hop_values],
                    op=mybir.AluOpType.add,
                )
            for first_hop, hops in runs:
                quantise_hops(neigh, n_codes, n_scales, first_hop, hops)

        def multiply_chunk(c):
            first = sum(CHUNK_SLOTS[:c])
            slots = CHUNK_SLOTS[c]
            x_codes, x_scales, n_codes, n_scales = packed[c]
            result = results_pool.tile([P, slots, HOPS, E], F32)

            def multiply(sums, h, s):
                place = (h + 1) % HOPS
                x_cols = slice((h * slots + s) * P, (h * slots + s + 1) * P)
                n_cols = slice((place * slots + s) * P, (place * slots + s + 1) * P)
                nc.tensor.matmul_mx(
                    out=sums,
                    lhsT=x_codes[:, x_cols].bitcast(FP8X4),
                    lhsT_scale=x_scales[:, x_cols],
                    rhs=w_codes[:, 0:E].bitcast(FP8X4),
                    rhs_scale=w_scales[:, 0:E],
                    start=True,
                    stop=False,
                )
                nc.tensor.matmul_mx(
                    out=sums,
                    lhsT=n_codes[:, n_cols].bitcast(FP8X4),
                    lhsT_scale=n_scales[:, n_cols],
                    rhs=w_codes[:, E : 2 * E].bitcast(FP8X4),
                    rhs_scale=w_scales[:, E : 2 * E],
                    start=False,
                    stop=True,
                )

            if c == MEANS_CHUNK:
                for s in range(slots):
                    sums = sums_pool.tile([P, LONG, E], F32)
                    for h in range(HOPS):
                        multiply(sums[:, h, :], h, s)
                    nc.scalar.copy(out=result[:, s, :, :], in_=sums[:, 0:HOPS, :])
                    nc.sync.dma_start(
                        out=out_view[:, first + s, :], in_=result[:, s, :, :].rearrange("q h e -> q (h e)")
                    )
                return
            for h in (2, 0, 1):
                sums = sums_pool.tile([P, LONG, E], F32)
                for s in range(slots):
                    multiply(sums[:, s, :], h, s)
                nc.scalar.copy(out=result[:, :, h, :], in_=sums[:, 0:slots, :])
            nc.sync.dma_start(
                out=out_view[:, first : first + slots, :],
                in_=result[:].rearrange("q s h e -> q s (h e)"),
            )

        w_rows = consts.tile([P, 2, PACK, E], BF16)
        for i, w in enumerate((w2a, w1a)):
            nc.sync.dma_start(
                out=w_rows[:, i, :, :].rearrange("r (u e) c -> r u (e c)", u=2),
                in_=w.rearrange("(u r e) c -> r u (e c)", u=2, e=2),
            )
        w_grouped = consts.tile([P, 2, E, PACK], BF16, align_bytes=64)
        nc.vector.tensor_copy(out=w_grouped[:], in_=w_rows[:].rearrange("r i t c -> r i c t"))
        w_codes = consts.tile([P, 2 * E], U32, align_bytes=64)
        w_scales = consts.tile([P, 2 * E], U8, align_bytes=64)
        nc.vector.quantize_mx(
            out=w_codes[:].bitcast(FP8X4),
            scales=w_scales[:],
            in_=w_grouped[:].rearrange("r i c t -> r (i c t)"),
        )
        ident = consts.tile([P, P], F32)
        make_identity(nc, ident[:])
        half_ident = consts.tile([P, P], BF16)
        nc.scalar.mul(out=half_ident[:], in_=ident[:], mul=0.5)

        load_chunk(0, 1)
        for c in range(1, LOAD_AHEAD):
            load_chunk(c, HOPS)
        for c in range(AHEAD):
            transpose_chunk(c)
        for c in range(CHUNKS):
            if c + LOAD_AHEAD < CHUNKS:
                load_chunk(c + LOAD_AHEAD, HOPS)
            if c + AHEAD < CHUNKS:
                transpose_chunk(c + AHEAD)
            quantise_chunk(c)
            multiply_chunk(c)
